import numpy as np
import ml_dtypes


BF16 = ml_dtypes.bfloat16


def bf(x):
    return np.asarray(x, np.float32).astype(BF16)


def f64(x):
    return np.asarray(x).astype(np.float64)


E2M1 = np.array([0.0, 0.5, 1.0, 1.5, 2.0, 3.0, 4.0, 6.0, -0.0, -0.5, -1.0, -1.5, -2.0, -3.0, -4.0, -6.0])


def pack_weight(w, fmt):
    k, n = w.shape
    w = f64(bf(w)).reshape(k // 32, 32, n)
    amax = np.abs(w).max(1)
    if fmt == "e4m3":
        byte = np.frexp(amax)[1] - 1 + 127 - 7
    else:
        mant, ex = np.frexp(amax / 6.0)
        byte = np.where(mant > 0.5, ex, ex - 1) + 127
    byte = np.clip(np.where(amax > 0, byte, 1), 1, 254)
    scaled = (w * np.exp2(127.0 - byte)[:, None, :]).reshape(k, n).astype(np.float32)
    by_word = np.ascontiguousarray(scaled.reshape(k // 512, 128, 4, n).transpose(0, 1, 3, 2))
    if fmt == "e4m3":
        words = by_word.astype(ml_dtypes.float8_e4m3fn).view(np.uint8)
    else:
        c = by_word.astype(ml_dtypes.float4_e2m1fn).view(np.uint8) & 0xF
        words = c[..., 0::2] | (c[..., 1::2] << 4)
    return np.ascontiguousarray(words), np.ascontiguousarray(byte.astype(np.uint8).reshape(k // 512, 16, n))


def unpack_weight(words, scales, fmt):
    g, p, n, _ = words.shape
    if fmt == "e4m3":
        vals = np.ascontiguousarray(words).view(ml_dtypes.float8_e4m3fn).astype(np.float64)
    else:
        nib = np.empty((g, p, n, 4), np.uint8)
        nib[..., 0::2] = words & 0xF
        nib[..., 1::2] = words >> 4
        vals = E2M1[nib]
    vals = vals * np.repeat(np.exp2(scales.astype(np.float64) - 127.0), 8, axis=1)[..., None]
    return vals.transpose(0, 1, 3, 2).reshape(g * 512, n)

def pack4(w):
    words, scales = pack_weight(w, "e2m1")
    return words.reshape(words.shape[0], 128, -1), scales


def unpack4(words, scales):
    return unpack_weight(words.reshape(words.shape[0], 128, -1, 2), scales, "e2m1")


def kspread(k):
    return np.exp2(np.repeat(np.random.randint(-6, 7, k // 32), 32).astype(np.float64))


T, B, I, H = 4, 128, 4096, 512


def sigmoid(v):
    return 1.0 / (1.0 + np.exp(-v))


def setup_inputs():
    s = kspread(I)
    input_seq = np.random.standard_normal((T, B, I)) * s
    input_seq_words, input_seq_scales = pack4(np.ascontiguousarray(input_seq.reshape(T * B, I).T))
    w = np.random.standard_normal((3 * H, I)) / np.sqrt(I) / s[None, :]
    words, scales = pack4(np.ascontiguousarray(w.T))
    b_ih = bf(np.random.standard_normal(3 * H) * 0.3)
    gh = bf(np.random.standard_normal((B, 3 * H)) * 0.5)
    return {"input_seq_words": input_seq_words,
            "input_seq_scales": input_seq_scales,
            "W_ih_words": words,
            "W_ih_scales": scales,
            "b_ih": b_ih,
            "gh": gh}


def reference(input_seq_words, input_seq_scales, W_ih_words, W_ih_scales, b_ih, gh):
    seq = unpack4(input_seq_words, input_seq_scales).T.reshape(T, B, I)
    gi = (seq @ unpack4(W_ih_words, W_ih_scales)) + f64(b_ih)
    g = f64(gh)
    i_r, i_z, i_n = gi[..., :H], gi[..., H:2 * H], gi[..., 2 * H:]
    h_r, h_z, h_n = g[..., :H], g[..., H:2 * H], g[..., 2 * H:]
    r = sigmoid(i_r + h_r)
    z = sigmoid(i_z + h_z)
    n = np.tanh(i_n + r * h_n)
    h = (1.0 - z) * n
    return np.transpose(h, (1, 0, 2))

@@ -1,0 +1,195 @@
+from contextlib import ExitStack
+
+import concourse.mybir as mybir
+
+FLOPS = 2 * 512 * 4096 * 1536
+
+F32 = mybir.dt.float32
+BF16 = mybir.dt.bfloat16
+I32 = mybir.dt.int32
+U8 = mybir.dt.uint8
+FP4X4 = mybir.dt.float4_e2m1fn_x4
+ACT = mybir.ActivationFunctionType
+ALU = mybir.AluOpType
+
+P = 128
+STEPS = 4
+H = 512
+PASSES = 8
+WARM_BEFORE = 2
+WARM_AFTER = 3
+
+X_CHUNKS = ((0, 1), (1, 2), (2, 4), (4, 6), (6, 8))
+WR_CHUNKS = ((0, 1), (1, 2), (2, 4), (4, 6), (6, 8))
+WZ_CHUNKS = ((0, 2), (2, 4), (4, 8))
+WN_CHUNKS = ((0, 4), (4, 8))
+CAND_GROUPS = ((0, 0, 512), (1, 0, 512), (2, 0, 256), (2, 256, 512), (3, 0, 256), (3, 256, 384), (3, 384, 512))
+Q_ORDER = (0, 2, 1, 3)
+
+
+def tile_grucellmodel_pa_kernel(tc, input_seq_words, input_seq_scales, W_ih_words, W_ih_scales, b_ih, gh, out):
+    nc = tc.nc
+
+    with ExitStack() as ctx:
+        keep = ctx.enter_context(tc.tile_pool(name="keep", bufs=1))
+        psum = ctx.enter_context(tc.psum_pool(name="psum", bufs=1))
+        ctx.enter_context(tc.manual_schedule())
+
+        def load_codes(words, col0, width, chunk, label):
+            g0, g1 = chunk
+            t = keep.tile([P, g1 - g0, width], U8, name="%s_%d" % (label, g0), align_bytes=64)
+            nc.sync.dma_start(
+                out=t[:].bitcast(I32),
+                in_=words[g0:g1, :, col0 : col0 + width].rearrange("g p n -> p g n").bitcast(I32),
+            )
+            return [(t, j) for j in range(g1 - g0)]
+
+        def new_plane(label):
+            t = keep.tile([P, PASSES, H], U8, name=label, align_bytes=64)
+            nc.vector.memset(t[:].bitcast(I32), 0)
+            return t
+
+        def load_plane(t, scales, col0):
+            for q in Q_ORDER:
+                nc.sync.dma_start(
+                    out=t[32 * q : 32 * q + 4, :, :].bitcast(I32),
+                    in_=scales[:, 4 * q : 4 * q + 4, col0 : col0 + H].rearrange("g r n -> r g n").bitcast(I32),
+                )
+
+        brow = keep.tile([P, 3 * H], BF16, name="brow")
+        nc.vector.memset(brow[:], 0.0)
+        nc.scalar.dma_start(out=brow[0:1, :], in_=b_ih.unsqueeze(0))
+
+        scr = keep.tile([P, 1], F32, name="scr")
+        scr2 = keep.tile([P, 1], F32, name="scr2")
+        nc.gpsimd.memset(scr[:], 0.0)
+        nc.scalar.activation(out=scr2[:], in_=scr[:], func=ACT.Sigmoid)
+
+        cx = []
+        cw = [[], [], []]
+        cx.extend(load_codes(input_seq_words, 0, 2 * H, X_CHUNKS[0], "cx"))
+        cw[0].extend(load_codes(W_ih_words, 0, 2 * H, WR_CHUNKS[0], "cwr"))
+        sx = new_plane("sx")
+        load_plane(sx, input_seq_scales, 0)
+        swr = new_plane("swr")
+        load_plane(swr, W_ih_scales, 0)
+
+        ones = keep.tile([P, H], BF16, name="ones")
+        nc.vector.memset(ones[:], 1.0)
+
+        for i in range(1, len(X_CHUNKS)):
+            cx.extend(load_codes(input_seq_words, 0, 2 * H, X_CHUNKS[i], "cx"))
+            cw[0].extend(load_codes(W_ih_words, 0, 2 * H, WR_CHUNKS[i], "cwr"))
+
+        gh_sb = keep.tile([P, 3 * H], BF16, name="gh_sb")
+        nc.sync.dma_start(out=gh_sb[:], in_=gh)
+
+        swz = new_plane("swz")
+        load_plane(swz, W_ih_scales, H)
+        for chunk in WZ_CHUNKS:
+            cw[1].extend(load_codes(W_ih_words, 2 * H, 2 * H, chunk, "cwz"))
+        swn = new_plane("swn")
+        load_plane(swn, W_ih_scales, 2 * H)
+        for chunk in WN_CHUNKS:
+            cw[2].extend(load_codes(W_ih_words, 4 * H, 2 * H, chunk, "cwn"))
+        sw = [swr, swz, swn]
+
+        warm_ps = psum.tile([P, H], F32, name="warm_ps", tag="bank7")
+        for i in range(WARM_BEFORE):
+            nc.tensor.matmul(out=warm_ps[:], lhsT=ones[:, 0:P], rhs=ones[:], start=True, stop=True)
+        bias_ps = []
+        for j in range(3):
+            bp = psum.tile([P, H], F32, name="bias_ps%d" % j, tag="bank%d" % (4 + j))
+            nc.tensor.matmul(out=bp[:], lhsT=ones[:, 0:P], rhs=brow[:, j * H : (j + 1) * H], start=True, stop=True)
+            bias_ps.append(bp)
+        for i in range(WARM_AFTER):
+            nc.tensor.matmul(out=warm_ps[:], lhsT=ones[:, 0:P], rhs=ones[:], start=True, stop=True)
+
+        bn = keep.tile([P, H], F32, name="bn")
+        nc.scalar.copy(out=bn[:], in_=bias_ps[2][:])
+        ghb = []
+        for j in range(2):
+            t = keep.tile([P, H], F32, name="ghb%d" % j)
+            nc.vector.tensor_tensor(out=t[:], in0=bias_ps[j][:], in1=gh_sb[:, j * H : (j + 1) * H], op=ALU.add)
+            ghb.append(t)
+
+        def mx(acc, gate, s, g, c0, c1):
+            xt, xj = cx[g]
+            wt, wj = cw[gate][g]
+            nc.tensor.matmul_mx(
+                out=acc[:],
+                lhsT=xt[:, xj, 2 * P * s : 2 * P * (s + 1)].bitcast(FP4X4),
+                lhsT_scale=sx[:, g, P * s : P * (s + 1)],
+                rhs=wt[:, wj, 2 * c0 : 2 * c1].bitcast(FP4X4),
+                rhs_scale=sw[gate][:, g, c0:c1],
+                start=(g == 0),
+                stop=(g == PASSES - 1),
+            )
+
+        def f32_tile(label):
+            return keep.tile([P, H], F32, name=label)
+
+        r_ps = [psum.tile([P, H], F32, name="r_ps%d" % s, tag="bank%d" % s) for s in range(STEPS)]
+        for g in range(PASSES):
+            for s in range(STEPS):
+                mx(r_ps[s], 0, s, g, 0, H)
+
+        r = []
+        for s in range(STEPS):
+            rp = f32_tile("rp%d" % s)
+            nc.vector.tensor_tensor(out=rp[:], in0=r_ps[s][:], in1=ghb[0][:], op=ALU.add)
+            rs = f32_tile("r%d" % s)
+            nc.scalar.activation(out=rs[:], in_=rp[:], func=ACT.Sigmoid)
+            r.append(rs)
+
+        t1 = [f32_tile("t1_%d" % s) for s in range(STEPS)]
+        t2 = [f32_tile("t2_%d" % s) for s in range(STEPS)]
+
+        def rh(s):
+            nc.vector.tensor_tensor(out=t1[s][:], in0=r[s][:], in1=gh_sb[:, 2 * H : 3 * H], op=ALU.mult)
+
+        def rhb(s):
+            nc.vector.tensor_tensor(out=t2[s][:], in0=t1[s][:], in1=bn[:], op=ALU.add)
+
+        rh(0)
+        for s in range(1, STEPS):
+            rh(s)
+            rhb(s - 1)
+        rhb(STEPS - 1)
+
+        z_ps = [psum.tile([P, H], F32, name="z_ps%d" % s, tag="bank%d" % (4 + s)) for s in range(STEPS)]
+        for g in range(PASSES):
+            for s in range(STEPS):
+                mx(z_ps[s], 1, s, g, 0, H)
+
+        zc = []
+        for s in range(STEPS):
+            zp = f32_tile("zp%d" % s)
+            nc.vector.tensor_tensor(out=zp[:], in0=z_ps[s][:], in1=ghb[1][:], op=ALU.add)
+            zs = f32_tile("zc%d" % s)
+            nc.scalar.activation(out=zs[:], in_=zp[:], func=ACT.Sigmoid, scale=-1.0)
+            zc.append(zs)
+
+        def cand_pre(acc, s, c0, c1):
+            w = c1 - c0
+            pre = keep.tile([P, w], F32, name="np%d_%d" % (s, c0))
+            nc.vector.tensor_tensor(out=pre[:], in0=acc[:], in1=t2[s][:, c0:c1], op=ALU.add)
+            cand = keep.tile([P, w], F32, name="n%d_%d" % (s, c0))
+            nc.scalar.activation(out=cand[:], in_=pre[:], func=ACT.Tanh)
+            return cand
+
+        def finish(cand, s, c0, c1):
+            h = keep.tile([P, c1 - c0], F32, name="h%d_%d" % (s, c0))
+            nc.vector.tensor_tensor(out=h[:], in0=zc[s][:, c0:c1], in1=cand[:], op=ALU.mult)
+            nc.sync.dma_start(out=out[:, s, c0:c1], in_=h[:])
+
+        waiting = None
+        for i, (s, c0, c1) in enumerate(CAND_GROUPS):
+            acc = psum.tile([P, c1 - c0], F32, name="n_ps%d" % i, tag="bank%d" % i)
+            for g in range(PASSES):
+                mx(acc, 2, s, g, c0, c1)
+            cand = cand_pre(acc, s, c0, c1)
+            if waiting is not None:
+                finish(*waiting)
+            waiting = (cand, s, c0, c1)
+        finish(*waiting)

@@ -16,8 +16,8 @@ P = 128
 STEPS = 4
 H = 512
 PASSES = 8
-WARM_BEFORE = 2
-WARM_AFTER = 3
+WARM_BEFORE = 4
+WARM_AFTER = 1
 
 X_CHUNKS = ((0, 1), (1, 2), (2, 4), (4, 6), (6, 8))
 WR_CHUNKS = ((0, 1), (1, 2), (2, 4), (4, 6), (6, 8))
@@ -57,8 +57,10 @@ def tile_grucellmodel_pa_kernel(tc, input_seq_words, input_seq_scales, W_ih_word
                 )
 
         brow = keep.tile([P, 3 * H], BF16, name="brow")
-        nc.vector.memset(brow[:], 0.0)
+        nc.vector.memset(brow[:].bitcast(I32), 0)
         nc.scalar.dma_start(out=brow[0:1, :], in_=b_ih.unsqueeze(0))
+        ones = keep.tile([P, H], BF16, name="ones")
+        nc.vector.memset(ones[:], 1.0)
 
         scr = keep.tile([P, 1], F32, name="scr")
         scr2 = keep.tile([P, 1], F32, name="scr2")
@@ -73,9 +75,6 @@ def tile_grucellmodel_pa_kernel(tc, input_seq_words, input_seq_scales, W_ih_word
         load_plane(sx, input_seq_scales, 0)
         swr = new_plane("swr")
         load_plane(swr, W_ih_scales, 0)
-
-        ones = keep.tile([P, H], BF16, name="ones")
-        nc.vector.memset(ones[:], 1.0)
 
         for i in range(1, len(X_CHUNKS)):
             cx.extend(load_codes(input_seq_words, 0, 2 * H, X_CHUNKS[i], "cx"))

@@ -16,15 +16,14 @@ P = 128
 STEPS = 4
 H = 512
 PASSES = 8
-WARM_BEFORE = 4
-WARM_AFTER = 1
+WARM_BEFORE = 2
+WARM_AFTER = 3
 
 X_CHUNKS = ((0, 1), (1, 2), (2, 4), (4, 6), (6, 8))
 WR_CHUNKS = ((0, 1), (1, 2), (2, 4), (4, 6), (6, 8))
 WZ_CHUNKS = ((0, 2), (2, 4), (4, 8))
 WN_CHUNKS = ((0, 4), (4, 8))
 CAND_GROUPS = ((0, 0, 512), (1, 0, 512), (2, 0, 256), (2, 256, 512), (3, 0, 256), (3, 256, 384), (3, 384, 512))
-Q_ORDER = (0, 2, 1, 3)
 
 
 def tile_grucellmodel_pa_kernel(tc, input_seq_words, input_seq_scales, W_ih_words, W_ih_scales, b_ih, gh, out):
@@ -44,54 +43,50 @@ def tile_grucellmodel_pa_kernel(tc, input_seq_words, input_seq_scales, W_ih_word
             )
             return [(t, j) for j in range(g1 - g0)]
 
-        def new_plane(label):
-            t = keep.tile([P, PASSES, H], U8, name=label, align_bytes=64)
+        def load_plane(scales, col0, g0, g1, label):
+            t = keep.tile([P, g1 - g0, H], U8, name=label, align_bytes=64)
             nc.vector.memset(t[:].bitcast(I32), 0)
-            return t
-
-        def load_plane(t, scales, col0):
-            for q in Q_ORDER:
+            for r in range(4):
                 nc.sync.dma_start(
-                    out=t[32 * q : 32 * q + 4, :, :].bitcast(I32),
-                    in_=scales[:, 4 * q : 4 * q + 4, col0 : col0 + H].rearrange("g r n -> r g n").bitcast(I32),
+                    out=t[r : P : 32, :, :].bitcast(I32),
+                    in_=scales[g0:g1, r : 16 : 4, col0 : col0 + H].rearrange("g q n -> q g n").bitcast(I32),
                 )
+            return [(t, j) for j in range(g1 - g0)]
 
         brow = keep.tile([P, 3 * H], BF16, name="brow")
-        nc.vector.memset(brow[:].bitcast(I32), 0)
-        nc.scalar.dma_start(out=brow[0:1, :], in_=b_ih.unsqueeze(0))
-        ones = keep.tile([P, H], BF16, name="ones")
-        nc.vector.memset(ones[:], 1.0)
-
-        scr = keep.tile([P, 1], F32, name="scr")
-        scr2 = keep.tile([P, 1], F32, name="scr2")
-        nc.gpsimd.memset(scr[:], 0.0)
-        nc.scalar.activation(out=scr2[:], in_=scr[:], func=ACT.Sigmoid)
+        nc.vector.memset(brow[:], 0.0)
 
         cx = []
         cw = [[], [], []]
         cx.extend(load_codes(input_seq_words, 0, 2 * H, X_CHUNKS[0], "cx"))
         cw[0].extend(load_codes(W_ih_words, 0, 2 * H, WR_CHUNKS[0], "cwr"))
-        sx = new_plane("sx")
-        load_plane(sx, input_seq_scales, 0)
-        swr = new_plane("swr")
-        load_plane(swr, W_ih_scales, 0)
+        nc.scalar.dma_start(out=brow[0:1, :], in_=b_ih.unsqueeze(0))
+        scr = keep.tile([P, 1], F32, name="scr")
+        scr2 = keep.tile([P, 1], F32, name="scr2")
+        nc.gpsimd.memset(scr[:], 0.0)
+        nc.scalar.activation(out=scr2[:], in_=scr[:], func=ACT.Sigmoid)
+        sx = load_plane(input_seq_scales, 0, 0, PASSES, "sx")
+        sw = [[], [], []]
+        sw[0].extend(load_plane(W_ih_scales, 0, 0, 4, "swr_a"))
+
+        ones = keep.tile([P, H], BF16, name="ones")
+        nc.vector.memset(ones[:], 1.0)
 
         for i in range(1, len(X_CHUNKS)):
+            if i == 3:
+                sw[0].extend(load_plane(W_ih_scales, 0, 4, PASSES, "swr_b"))
             cx.extend(load_codes(input_seq_words, 0, 2 * H, X_CHUNKS[i], "cx"))
             cw[0].extend(load_codes(W_ih_words, 0, 2 * H, WR_CHUNKS[i], "cwr"))
 
         gh_sb = keep.tile([P, 3 * H], BF16, name="gh_sb")
         nc.sync.dma_start(out=gh_sb[:], in_=gh)
 
-        swz = new_plane("swz")
-        load_plane(swz, W_ih_scales, H)
+        sw[1].extend(load_plane(W_ih_scales, H, 0, PASSES, "swz"))
         for chunk in WZ_CHUNKS:
             cw[1].extend(load_codes(W_ih_words, 2 * H, 2 * H, chunk, "cwz"))
-        swn = new_plane("swn")
-        load_plane(swn, W_ih_scales, 2 * H)
+        sw[2].extend(load_plane(W_ih_scales, 2 * H, 0, PASSES, "swn"))
         for chunk in WN_CHUNKS:
             cw[2].extend(load_codes(W_ih_words, 4 * H, 2 * H, chunk, "cwn"))
-        sw = [swr, swz, swn]
 
         warm_ps = psum.tile([P, H], F32, name="warm_ps", tag="bank7")
         for i in range(WARM_BEFORE):
@@ -115,12 +110,14 @@ def tile_grucellmodel_pa_kernel(tc, input_seq_words, input_seq_scales, W_ih_word
         def mx(acc, gate, s, g, c0, c1):
             xt, xj = cx[g]
             wt, wj = cw[gate][g]
+            sxt, sxj = sx[g]
+            swt, swj = sw[gate][g]
             nc.tensor.matmul_mx(
                 out=acc[:],
                 lhsT=xt[:, xj, 2 * P * s : 2 * P * (s + 1)].bitcast(FP4X4),
-                lhsT_scale=sx[:, g, P * s : P * (s + 1)],
+                lhsT_scale=sxt[:, sxj, P * s : P * (s + 1)],
                 rhs=wt[:, wj, 2 * c0 : 2 * c1].bitcast(FP4X4),
-                rhs_scale=sw[gate][:, g, c0:c1],
+                rhs_scale=swt[:, swj, c0:c1],
                 start=(g == 0),
                 stop=(g == PASSES - 1),
             )

@@ -16,7 +16,7 @@ P = 128
 STEPS = 4
 H = 512
 PASSES = 8
-WARM_BEFORE = 2
+WARM_BEFORE = 4
 WARM_AFTER = 3
 
 X_CHUNKS = ((0, 1), (1, 2), (2, 4), (4, 6), (6, 8))
@@ -55,6 +55,8 @@ def tile_grucellmodel_pa_kernel(tc, input_seq_words, input_seq_scales, W_ih_word
 
         brow = keep.tile([P, 3 * H], BF16, name="brow")
         nc.vector.memset(brow[:], 0.0)
+        ones = keep.tile([P, H], BF16, name="ones")
+        nc.vector.memset(ones[:], 1.0)
 
         cx = []
         cw = [[], [], []]
@@ -68,9 +70,6 @@ def tile_grucellmodel_pa_kernel(tc, input_seq_words, input_seq_scales, W_ih_word
         sx = load_plane(input_seq_scales, 0, 0, PASSES, "sx")
         sw = [[], [], []]
         sw[0].extend(load_plane(W_ih_scales, 0, 0, 4, "swr_a"))
-
-        ones = keep.tile([P, H], BF16, name="ones")
-        nc.vector.memset(ones[:], 1.0)
 
         for i in range(1, len(X_CHUNKS)):
             if i == 3:

@@ -36,7 +36,7 @@ def tile_grucellmodel_pa_kernel(tc, input_seq_words, input_seq_scales, W_ih_word
 
         def load_codes(words, col0, width, chunk, label):
             g0, g1 = chunk
-            t = keep.tile([P, g1 - g0, width], U8, name="%s_%d" % (label, g0), align_bytes=64)
+            t = keep.tile([P, g1 - g0, width], U8, name="%s_%d" % (label, g0), align_bytes=256)
             nc.sync.dma_start(
                 out=t[:].bitcast(I32),
                 in_=words[g0:g1, :, col0 : col0 + width].rearrange("g p n -> p g n").bitcast(I32),
@@ -44,7 +44,7 @@ def tile_grucellmodel_pa_kernel(tc, input_seq_words, input_seq_scales, W_ih_word
             return [(t, j) for j in range(g1 - g0)]
 
         def load_plane(scales, col0, g0, g1, label):
-            t = keep.tile([P, g1 - g0, H], U8, name=label, align_bytes=64)
+            t = keep.tile([P, g1 - g0, H], U8, name=label, align_bytes=256)
             nc.vector.memset(t[:].bitcast(I32), 0)
             for r in range(4):
                 nc.sync.dma_start(

@@ -153,8 +153,8 @@ def tile_grucellmodel_pa_kernel(tc, input_seq_words, input_seq_scales, W_ih_word
         rhb(STEPS - 1)
 
         z_ps = [psum.tile([P, H], F32, name="z_ps%d" % s, tag="bank%d" % (4 + s)) for s in range(STEPS)]
-        for g in range(PASSES):
-            for s in range(STEPS):
+        for s in range(STEPS):
+            for g in range(PASSES):
                 mx(z_ps[s], 1, s, g, 0, H)
 
         zc = []

@@ -16,13 +16,9 @@ P = 128
 STEPS = 4
 H = 512
 PASSES = 8
+EARLY = 2
 WARM_BEFORE = 4
-WARM_AFTER = 3
 
-X_CHUNKS = ((0, 1), (1, 2), (2, 4), (4, 6), (6, 8))
-WR_CHUNKS = ((0, 1), (1, 2), (2, 4), (4, 6), (6, 8))
-WZ_CHUNKS = ((0, 2), (2, 4), (4, 8))
-WN_CHUNKS = ((0, 4), (4, 8))
 CAND_GROUPS = ((0, 0, 512), (1, 0, 512), (2, 0, 256), (2, 256, 512), (3, 0, 256), (3, 256, 384), (3, 384, 512))
 
 
@@ -34,58 +30,87 @@ def tile_grucellmodel_pa_kernel(tc, input_seq_words, input_seq_scales, W_ih_word
         psum = ctx.enter_context(tc.psum_pool(name="psum", bufs=1))
         ctx.enter_context(tc.manual_schedule())
 
-        def load_codes(words, col0, width, chunk, label):
-            g0, g1 = chunk
+        cx = [None] * PASSES
+        sx = [None] * PASSES
+        cw = [[None] * PASSES for gate in range(3)]
+        sw = [[None] * PASSES for gate in range(3)]
+
+        def load_codes(words, col0, width, g0, g1, label):
             t = keep.tile([P, g1 - g0, width], U8, name="%s_%d" % (label, g0), align_bytes=256)
             nc.sync.dma_start(
                 out=t[:].bitcast(I32),
                 in_=words[g0:g1, :, col0 : col0 + width].rearrange("g p n -> p g n").bitcast(I32),
             )
-            return [(t, j) for j in range(g1 - g0)]
+            return t
 
-        def load_plane(scales, col0, g0, g1, label):
-            t = keep.tile([P, g1 - g0, H], U8, name=label, align_bytes=256)
+        def load_x(g0, g1):
+            t = load_codes(input_seq_words, 0, 2 * H, g0, g1, "cx")
+            for g in range(g0, g1):
+                cx[g] = (t, g - g0)
+
+        def load_w(gate0, gates, g0, g1):
+            t = load_codes(W_ih_words, 2 * H * gate0, 2 * H * gates, g0, g1, "cw%d" % gate0)
+            for gate in range(gate0, gate0 + gates):
+                for g in range(g0, g1):
+                    cw[gate][g] = (t, g - g0, 2 * H * (gate - gate0))
+
+        def load_plane(scales, col0, width, g0, g1, label):
+            t = keep.tile([P, g1 - g0, width], U8, name=label, align_bytes=256)
             nc.vector.memset(t[:].bitcast(I32), 0)
             for r in range(4):
                 nc.sync.dma_start(
                     out=t[r : P : 32, :, :].bitcast(I32),
-                    in_=scales[g0:g1, r : 16 : 4, col0 : col0 + H].rearrange("g q n -> q g n").bitcast(I32),
+                    in_=scales[g0:g1, r : 16 : 4, col0 : col0 + width].rearrange("g q n -> q g n").bitcast(I32),
                 )
-            return [(t, j) for j in range(g1 - g0)]
+            return t
+
+        def load_sx(g0, g1):
+            t = load_plane(input_seq_scales, 0, H, g0, g1, "sx_%d" % g0)
+            for g in range(g0, g1):
+                sx[g] = (t, g - g0)
+
+        def load_sw(gate0, gates, g0, g1):
+            t = load_plane(W_ih_scales, H * gate0, H * gates, g0, g1, "sw%d_%d" % (gate0, g0))
+            for gate in range(gate0, gate0 + gates):
+                for g in range(g0, g1):
+                    sw[gate][g] = (t, g - g0, H * (gate - gate0))
 
         brow = keep.tile([P, 3 * H], BF16, name="brow")
         nc.vector.memset(brow[:], 0.0)
         ones = keep.tile([P, H], BF16, name="ones")
         nc.vector.memset(ones[:], 1.0)
 
-        cx = []
-        cw = [[], [], []]
-        cx.extend(load_codes(input_seq_words, 0, 2 * H, X_CHUNKS[0], "cx"))
-        cw[0].extend(load_codes(W_ih_words, 0, 2 * H, WR_CHUNKS[0], "cwr"))
+        load_x(0, 1)
+        load_w(0, 1, 0, 1)
         nc.scalar.dma_start(out=brow[0:1, :], in_=b_ih.unsqueeze(0))
         scr = keep.tile([P, 1], F32, name="scr")
         scr2 = keep.tile([P, 1], F32, name="scr2")
         nc.gpsimd.memset(scr[:], 0.0)
         nc.scalar.activation(out=scr2[:], in_=scr[:], func=ACT.Sigmoid)
-        sx = load_plane(input_seq_scales, 0, 0, PASSES, "sx")
-        sw = [[], [], []]
-        sw[0].extend(load_plane(W_ih_scales, 0, 0, 4, "swr_a"))
+        load_sx(0, EARLY)
+        load_sw(0, 2, 0, EARLY)
 
-        for i in range(1, len(X_CHUNKS)):
-            if i == 3:
-                sw[0].extend(load_plane(W_ih_scales, 0, 4, PASSES, "swr_b"))
-            cx.extend(load_codes(input_seq_words, 0, 2 * H, X_CHUNKS[i], "cx"))
-            cw[0].extend(load_codes(W_ih_words, 0, 2 * H, WR_CHUNKS[i], "cwr"))
+        load_w(1, 1, 0, 1)
+        load_x(1, 2)
+        load_w(0, 2, 1, 2)
+        load_x(2, 4)
+        load_w(0, 1, 2, 4)
+        load_sx(EARLY, PASSES)
+        load_sw(0, 1, EARLY, PASSES)
+        load_x(4, 6)
+        load_w(0, 1, 4, 6)
+        load_x(6, 8)
+        load_w(0, 1, 6, 8)
 
         gh_sb = keep.tile([P, 3 * H], BF16, name="gh_sb")
         nc.sync.dma_start(out=gh_sb[:], in_=gh)
 
-        sw[1].extend(load_plane(W_ih_scales, H, 0, PASSES, "swz"))
-        for chunk in WZ_CHUNKS:
-            cw[1].extend(load_codes(W_ih_words, 2 * H, 2 * H, chunk, "cwz"))
-        sw[2].extend(load_plane(W_ih_scales, 2 * H, 0, PASSES, "swn"))
-        for chunk in WN_CHUNKS:
-            cw[2].extend(load_codes(W_ih_words, 4 * H, 2 * H, chunk, "cwn"))
+        load_sw(1, 1, EARLY, PASSES)
+        load_w(1, 1, 2, 4)
+        load_w(1, 1, 4, 8)
+        load_sw(2, 1, 0, PASSES)
+        load_w(2, 1, 0, 4)
+        load_w(2, 1, 4, 8)
 
         warm_ps = psum.tile([P, H], F32, name="warm_ps", tag="bank7")
         for i in range(WARM_BEFORE):
@@ -95,28 +120,24 @@ def tile_grucellmodel_pa_kernel(tc, input_seq_words, input_seq_scales, W_ih_word
             bp = psum.tile([P, H], F32, name="bias_ps%d" % j, tag="bank%d" % (4 + j))
             nc.tensor.matmul(out=bp[:], lhsT=ones[:, 0:P], rhs=brow[:, j * H : (j + 1) * H], start=True, stop=True)
             bias_ps.append(bp)
-        for i in range(WARM_AFTER):
-            nc.tensor.matmul(out=warm_ps[:], lhsT=ones[:, 0:P], rhs=ones[:], start=True, stop=True)
 
-        bn = keep.tile([P, H], F32, name="bn")
-        nc.scalar.copy(out=bn[:], in_=bias_ps[2][:])
-        ghb = []
-        for j in range(2):
-            t = keep.tile([P, H], F32, name="ghb%d" % j)
-            nc.vector.tensor_tensor(out=t[:], in0=bias_ps[j][:], in1=gh_sb[:, j * H : (j + 1) * H], op=ALU.add)
-            ghb.append(t)
+        b_sb = [keep.tile([P, H], F32, name="b_sb%d" % j) for j in range(3)]
+        nc.scalar.copy(out=b_sb[0][:], in_=bias_ps[0][:])
+        nc.vector.tensor_copy(out=b_sb[1][:], in_=bias_ps[1][:])
+        nc.scalar.copy(out=b_sb[2][:], in_=bias_ps[2][:])
+        bn = b_sb[2]
 
         def mx(acc, gate, s, g, c0, c1):
             xt, xj = cx[g]
-            wt, wj = cw[gate][g]
+            wt, wj, wo = cw[gate][g]
             sxt, sxj = sx[g]
-            swt, swj = sw[gate][g]
+            swt, swj, so = sw[gate][g]
             nc.tensor.matmul_mx(
                 out=acc[:],
                 lhsT=xt[:, xj, 2 * P * s : 2 * P * (s + 1)].bitcast(FP4X4),
                 lhsT_scale=sxt[:, sxj, P * s : P * (s + 1)],
-                rhs=wt[:, wj, 2 * c0 : 2 * c1].bitcast(FP4X4),
-                rhs_scale=swt[:, swj, c0:c1],
+                rhs=wt[:, wj, wo + 2 * c0 : wo + 2 * c1].bitcast(FP4X4),
+                rhs_scale=swt[:, swj, so + c0 : so + c1],
                 start=(g == 0),
                 stop=(g == PASSES - 1),
             )
@@ -125,9 +146,19 @@ def tile_grucellmodel_pa_kernel(tc, input_seq_words, input_seq_scales, W_ih_word
             return keep.tile([P, H], F32, name=label)
 
         r_ps = [psum.tile([P, H], F32, name="r_ps%d" % s, tag="bank%d" % s) for s in range(STEPS)]
+        z_ps = [psum.tile([P, H], F32, name="z_ps%d" % s, tag="bank%d" % (4 + s)) for s in range(STEPS)]
         for g in range(PASSES):
             for s in range(STEPS):
                 mx(r_ps[s], 0, s, g, 0, H)
+            if g < EARLY:
+                for s in range(STEPS):
+                    mx(z_ps[s], 1, s, g, 0, H)
+
+        ghb = []
+        for j in range(2):
+            t = keep.tile([P, H], F32, name="ghb%d" % j)
+            nc.vector.tensor_tensor(out=t[:], in0=b_sb[j][:], in1=gh_sb[:, j * H : (j + 1) * H], op=ALU.add)
+            ghb.append(t)
 
         r = []
         for s in range(STEPS):
@@ -152,9 +183,8 @@ def tile_grucellmodel_pa_kernel(tc, input_seq_words, input_seq_scales, W_ih_word
             rhb(s - 1)
         rhb(STEPS - 1)
 
-        z_ps = [psum.tile([P, H], F32, name="z_ps%d" % s, tag="bank%d" % (4 + s)) for s in range(STEPS)]
         for s in range(STEPS):
-            for g in range(PASSES):
+            for g in range(EARLY, PASSES):
                 mx(z_ps[s], 1, s, g, 0, H)
 
         zc = []

@@ -17,7 +17,7 @@ STEPS = 4
 H = 512
 PASSES = 8
 EARLY = 2
-WARM_BEFORE = 4
+WARM_BEFORE = 16
 
 CAND_GROUPS = ((0, 0, 512), (1, 0, 512), (2, 0, 256), (2, 256, 512), (3, 0, 256), (3, 256, 384), (3, 384, 512))
 
@@ -75,10 +75,10 @@ def tile_grucellmodel_pa_kernel(tc, input_seq_words, input_seq_scales, W_ih_word
                 for g in range(g0, g1):
                     sw[gate][g] = (t, g - g0, H * (gate - gate0))
 
+        ones = keep.tile([P, P], BF16, name="ones")
+        nc.vector.memset(ones[:], 1.0)
         brow = keep.tile([P, 3 * H], BF16, name="brow")
         nc.vector.memset(brow[:], 0.0)
-        ones = keep.tile([P, H], BF16, name="ones")
-        nc.vector.memset(ones[:], 1.0)
 
         load_x(0, 1)
         load_w(0, 1, 0, 1)
@@ -114,11 +114,11 @@ def tile_grucellmodel_pa_kernel(tc, input_seq_words, input_seq_scales, W_ih_word
 
         warm_ps = psum.tile([P, H], F32, name="warm_ps", tag="bank7")
         for i in range(WARM_BEFORE):
-            nc.tensor.matmul(out=warm_ps[:], lhsT=ones[:, 0:P], rhs=ones[:], start=True, stop=True)
+            nc.tensor.matmul(out=warm_ps[:, 0:P], lhsT=ones[:], rhs=ones[:], start=True, stop=True)
         bias_ps = []
         for j in range(3):
             bp = psum.tile([P, H], F32, name="bias_ps%d" % j, tag="bank%d" % (4 + j))
-            nc.tensor.matmul(out=bp[:], lhsT=ones[:, 0:P], rhs=brow[:, j * H : (j + 1) * H], start=True, stop=True)
+            nc.tensor.matmul(out=bp[:], lhsT=ones[:], rhs=brow[:, j * H : (j + 1) * H], start=True, stop=True)
             bias_ps.append(bp)
 
         b_sb = [keep.tile([P, H], F32, name="b_sb%d" % j) for j in range(3)]

@@ -17,6 +17,7 @@ STEPS = 4
 H = 512
 PASSES = 8
 EARLY = 2
+STREAMED = 4
 WARM_BEFORE = 16
 
 CAND_GROUPS = ((0, 0, 512), (1, 0, 512), (2, 0, 256), (2, 256, 512), (3, 0, 256), (3, 256, 384), (3, 384, 512))
@@ -147,12 +148,15 @@ def tile_grucellmodel_pa_kernel(tc, input_seq_words, input_seq_scales, W_ih_word
 
         r_ps = [psum.tile([P, H], F32, name="r_ps%d" % s, tag="bank%d" % s) for s in range(STEPS)]
         z_ps = [psum.tile([P, H], F32, name="z_ps%d" % s, tag="bank%d" % (4 + s)) for s in range(STEPS)]
-        for g in range(PASSES):
+        for g in range(STREAMED):
             for s in range(STEPS):
                 mx(r_ps[s], 0, s, g, 0, H)
             if g < EARLY:
                 for s in range(STEPS):
                     mx(z_ps[s], 1, s, g, 0, H)
+        for s in range(STEPS):
+            for g in range(STREAMED, PASSES):
+                mx(r_ps[s], 0, s, g, 0, H)
 
         ghb = []
         for j in range(2):
@@ -161,7 +165,8 @@ def tile_grucellmodel_pa_kernel(tc, input_seq_words, input_seq_scales, W_ih_word
             ghb.append(t)
 
         r = []
-        for s in range(STEPS):
+
+        def reset_gate(s):
             rp = f32_tile("rp%d" % s)
             nc.vector.tensor_tensor(out=rp[:], in0=r_ps[s][:], in1=ghb[0][:], op=ALU.add)
             rs = f32_tile("r%d" % s)
@@ -177,10 +182,14 @@ def tile_grucellmodel_pa_kernel(tc, input_seq_words, input_seq_scales, W_ih_word
         def rhb(s):
             nc.vector.tensor_tensor(out=t2[s][:], in0=t1[s][:], in1=bn[:], op=ALU.add)
 
-        rh(0)
+        reset_gate(0)
         for s in range(1, STEPS):
-            rh(s)
-            rhb(s - 1)
+            reset_gate(s)
+            rh(s - 1)
+            if s >= 2:
+                rhb(s - 2)
+        rh(STEPS - 1)
+        rhb(STEPS - 2)
         rhb(STEPS - 1)
 
         for s in range(STEPS):

@@ -55,41 +55,54 @@ def tile_grucellmodel_pa_kernel(tc, input_seq_words, input_seq_scales, W_ih_word
                 for g in range(g0, g1):
                     cw[gate][g] = (t, g - g0, 2 * H * (gate - gate0))
 
-        def load_plane(scales, col0, width, g0, g1, label):
+        def zeroed_plane(width, g0, g1, label):
             t = keep.tile([P, g1 - g0, width], U8, name=label, align_bytes=256)
             nc.vector.memset(t[:].bitcast(I32), 0)
-            for r in range(4):
+            return t
+
+        def fill_plane(t, scales, col0, width, g0, g1, rows):
+            for r in rows:
                 nc.sync.dma_start(
                     out=t[r : P : 32, :, :].bitcast(I32),
                     in_=scales[g0:g1, r : 16 : 4, col0 : col0 + width].rearrange("g q n -> q g n").bitcast(I32),
                 )
-            return t
 
-        def load_sx(g0, g1):
-            t = load_plane(input_seq_scales, 0, H, g0, g1, "sx_%d" % g0)
+        def zeroed_sx(g0, g1):
+            t = zeroed_plane(H, g0, g1, "sx_%d" % g0)
             for g in range(g0, g1):
                 sx[g] = (t, g - g0)
+            return t
 
-        def load_sw(gate0, gates, g0, g1):
-            t = load_plane(W_ih_scales, H * gate0, H * gates, g0, g1, "sw%d_%d" % (gate0, g0))
+        def zeroed_sw(gate0, gates, g0, g1):
+            t = zeroed_plane(H * gates, g0, g1, "sw%d_%d" % (gate0, g0))
             for gate in range(gate0, gate0 + gates):
                 for g in range(g0, g1):
                     sw[gate][g] = (t, g - g0, H * (gate - gate0))
+            return t
+
+        def load_sx(g0, g1):
+            fill_plane(zeroed_sx(g0, g1), input_seq_scales, 0, H, g0, g1, range(4))
+
+        def load_sw(gate0, gates, g0, g1):
+            fill_plane(zeroed_sw(gate0, gates, g0, g1), W_ih_scales, H * gate0, H * gates, g0, g1, range(4))
 
         ones = keep.tile([P, P], BF16, name="ones")
         nc.vector.memset(ones[:], 1.0)
+        sx_first = zeroed_sx(0, EARLY)
         brow = keep.tile([P, 3 * H], BF16, name="brow")
         nc.vector.memset(brow[:], 0.0)
+        sw_first = zeroed_sw(0, 2, 0, EARLY)
 
         load_x(0, 1)
         load_w(0, 1, 0, 1)
+        fill_plane(sx_first, input_seq_scales, 0, H, 0, EARLY, range(4))
+        fill_plane(sw_first, W_ih_scales, 0, 2 * H, 0, EARLY, range(1))
         nc.scalar.dma_start(out=brow[0:1, :], in_=b_ih.unsqueeze(0))
         scr = keep.tile([P, 1], F32, name="scr")
         scr2 = keep.tile([P, 1], F32, name="scr2")
         nc.gpsimd.memset(scr[:], 0.0)
         nc.scalar.activation(out=scr2[:], in_=scr[:], func=ACT.Sigmoid)
-        load_sx(0, EARLY)
-        load_sw(0, 2, 0, EARLY)
+        fill_plane(sw_first, W_ih_scales, 0, 2 * H, 0, EARLY, range(1, 4))
 
         load_w(1, 1, 0, 1)
         load_x(1, 2)

@@ -107,10 +107,10 @@ def tile_grucellmodel_pa_kernel(tc, input_seq_words, input_seq_scales, W_ih_word
         load_w(1, 1, 0, 1)
         load_x(1, 2)
         load_w(0, 2, 1, 2)
-        load_x(2, 4)
-        load_w(0, 1, 2, 4)
         load_sx(EARLY, PASSES)
         load_sw(0, 1, EARLY, PASSES)
+        load_x(2, 4)
+        load_w(0, 1, 2, 4)
         load_x(4, 6)
         load_w(0, 1, 4, 6)
         load_x(6, 8)

@@ -205,8 +205,11 @@ def tile_grucellmodel_pa_kernel(tc, input_seq_words, input_seq_scales, W_ih_word
         rhb(STEPS - 2)
         rhb(STEPS - 1)
 
+        for g in range(EARLY, STREAMED):
+            for s in range(STEPS):
+                mx(z_ps[s], 1, s, g, 0, H)
         for s in range(STEPS):
-            for g in range(EARLY, PASSES):
+            for g in range(STREAMED, PASSES):
                 mx(z_ps[s], 1, s, g, 0, H)
 
         zc = []

@@ -88,14 +88,14 @@ def tile_grucellmodel_pa_kernel(tc, input_seq_words, input_seq_scales, W_ih_word
 
         ones = keep.tile([P, P], BF16, name="ones")
         nc.vector.memset(ones[:], 1.0)
-        sx_first = zeroed_sx(0, EARLY)
+        sx_first = zeroed_sx(0, STREAMED)
         brow = keep.tile([P, 3 * H], BF16, name="brow")
         nc.vector.memset(brow[:], 0.0)
         sw_first = zeroed_sw(0, 2, 0, EARLY)
 
         load_x(0, 1)
         load_w(0, 1, 0, 1)
-        fill_plane(sx_first, input_seq_scales, 0, H, 0, EARLY, range(4))
+        fill_plane(sx_first, input_seq_scales, 0, H, 0, STREAMED, range(4))
         fill_plane(sw_first, W_ih_scales, 0, 2 * H, 0, EARLY, range(1))
         nc.scalar.dma_start(out=brow[0:1, :], in_=b_ih.unsqueeze(0))
         scr = keep.tile([P, 1], F32, name="scr")
@@ -107,10 +107,10 @@ def tile_grucellmodel_pa_kernel(tc, input_seq_words, input_seq_scales, W_ih_word
         load_w(1, 1, 0, 1)
         load_x(1, 2)
         load_w(0, 2, 1, 2)
-        load_sx(EARLY, PASSES)
         load_sw(0, 1, EARLY, PASSES)
         load_x(2, 4)
         load_w(0, 1, 2, 4)
+        load_sx(STREAMED, PASSES)
         load_x(4, 6)
         load_w(0, 1, 4, 6)
         load_x(6, 8)

@@ -17,6 +17,7 @@ STEPS = 4
 H = 512
 PASSES = 8
 EARLY = 2
+X_FIRST = 3
 STREAMED = 4
 WARM_BEFORE = 16
 
@@ -86,16 +87,16 @@ def tile_grucellmodel_pa_kernel(tc, input_seq_words, input_seq_scales, W_ih_word
         def load_sw(gate0, gates, g0, g1):
             fill_plane(zeroed_sw(gate0, gates, g0, g1), W_ih_scales, H * gate0, H * gates, g0, g1, range(4))
 
+        sx_first = zeroed_sx(0, X_FIRST)
         ones = keep.tile([P, P], BF16, name="ones")
         nc.vector.memset(ones[:], 1.0)
-        sx_first = zeroed_sx(0, STREAMED)
         brow = keep.tile([P, 3 * H], BF16, name="brow")
-        nc.vector.memset(brow[:], 0.0)
+        nc.vector.memset(brow[:].bitcast(I32), 0)
         sw_first = zeroed_sw(0, 2, 0, EARLY)
 
         load_x(0, 1)
         load_w(0, 1, 0, 1)
-        fill_plane(sx_first, input_seq_scales, 0, H, 0, STREAMED, range(4))
+        fill_plane(sx_first, input_seq_scales, 0, H, 0, X_FIRST, range(4))
         fill_plane(sw_first, W_ih_scales, 0, 2 * H, 0, EARLY, range(1))
         nc.scalar.dma_start(out=brow[0:1, :], in_=b_ih.unsqueeze(0))
         scr = keep.tile([P, 1], F32, name="scr")
@@ -110,7 +111,7 @@ def tile_grucellmodel_pa_kernel(tc, input_seq_words, input_seq_scales, W_ih_word
         load_sw(0, 1, EARLY, PASSES)
         load_x(2, 4)
         load_w(0, 1, 2, 4)
-        load_sx(STREAMED, PASSES)
+        load_sx(X_FIRST, PASSES)
         load_x(4, 6)
         load_w(0, 1, 4, 6)
         load_x(6, 8)

from contextlib import ExitStack

import concourse.mybir as mybir

FLOPS = 2 * 512 * 4096 * 1536

F32 = mybir.dt.float32
BF16 = mybir.dt.bfloat16
I32 = mybir.dt.int32
U8 = mybir.dt.uint8
FP4X4 = mybir.dt.float4_e2m1fn_x4
ACT = mybir.ActivationFunctionType
ALU = mybir.AluOpType

P = 128
STEPS = 4
H = 512
PASSES = 8
EARLY = 2
X_FIRST = 3
STREAMED = 4
WARM_BEFORE = 16

CAND_GROUPS = ((0, 0, 512), (1, 0, 512), (2, 0, 256), (2, 256, 512), (3, 0, 256), (3, 256, 384), (3, 384, 512))


def tile_grucellmodel_pa_kernel(tc, input_seq_words, input_seq_scales, W_ih_words, W_ih_scales, b_ih, gh, out):
    nc = tc.nc

    with ExitStack() as ctx:
        keep = ctx.enter_context(tc.tile_pool(name="keep", bufs=1))
        psum = ctx.enter_context(tc.psum_pool(name="psum", bufs=1))
        ctx.enter_context(tc.manual_schedule())

        cx = [None] * PASSES
        sx = [None] * PASSES
        cw = [[None] * PASSES for gate in range(3)]
        sw = [[None] * PASSES for gate in range(3)]

        def load_codes(words, col0, width, g0, g1, label):
            t = keep.tile([P, g1 - g0, width], U8, name="%s_%d" % (label, g0), align_bytes=256)
            nc.sync.dma_start(
                out=t[:].bitcast(I32),
                in_=words[g0:g1, :, col0 : col0 + width].rearrange("g p n -> p g n").bitcast(I32),
            )
            return t

        def load_x(g0, g1):
            t = load_codes(input_seq_words, 0, 2 * H, g0, g1, "cx")
            for g in range(g0, g1):
                cx[g] = (t, g - g0)

        def load_w(gate0, gates, g0, g1):
            t = load_codes(W_ih_words, 2 * H * gate0, 2 * H * gates, g0, g1, "cw%d" % gate0)
            for gate in range(gate0, gate0 + gates):
                for g in range(g0, g1):
                    cw[gate][g] = (t, g - g0, 2 * H * (gate - gate0))

        def zeroed_plane(width, g0, g1, label):
            t = keep.tile([P, g1 - g0, width], U8, name=label, align_bytes=256)
            nc.vector.memset(t[:].bitcast(I32), 0)
            return t

        def fill_plane(t, scales, col0, width, g0, g1, rows):
            for r in rows:
                nc.sync.dma_start(
                    out=t[r : P : 32, :, :].bitcast(I32),
                    in_=scales[g0:g1, r : 16 : 4, col0 : col0 + width].rearrange("g q n -> q g n").bitcast(I32),
                )

        def zeroed_sx(g0, g1):
            t = zeroed_plane(H, g0, g1, "sx_%d" % g0)
            for g in range(g0, g1):
                sx[g] = (t, g - g0)
            return t

        def zeroed_sw(gate0, gates, g0, g1):
            t = zeroed_plane(H * gates, g0, g1, "sw%d_%d" % (gate0, g0))
            for gate in range(gate0, gate0 + gates):
                for g in range(g0, g1):
                    sw[gate][g] = (t, g - g0, H * (gate - gate0))
            return t

        def load_sx(g0, g1):
            fill_plane(zeroed_sx(g0, g1), input_seq_scales, 0, H, g0, g1, range(4))

        def load_sw(gate0, gates, g0, g1):
            fill_plane(zeroed_sw(gate0, gates, g0, g1), W_ih_scales, H * gate0, H * gates, g0, g1, range(4))

        sx_first = zeroed_sx(0, X_FIRST)
        ones = keep.tile([P, P], BF16, name="ones")
        nc.vector.memset(ones[:], 1.0)
        brow = keep.tile([P, 3 * H], BF16, name="brow")
        nc.vector.memset(brow[:].bitcast(I32), 0)
        sw_first = zeroed_sw(0, 2, 0, EARLY)

        load_x(0, 1)
        load_w(0, 1, 0, 1)
        fill_plane(sx_first, input_seq_scales, 0, H, 0, X_FIRST, range(4))
        fill_plane(sw_first, W_ih_scales, 0, 2 * H, 0, EARLY, range(1))
        nc.scalar.dma_start(out=brow[0:1, :], in_=b_ih.unsqueeze(0))
        scr = keep.tile([P, 1], F32, name="scr")
        scr2 = keep.tile([P, 1], F32, name="scr2")
        nc.gpsimd.memset(scr[:], 0.0)
        nc.scalar.activation(out=scr2[:], in_=scr[:], func=ACT.Sigmoid)
        fill_plane(sw_first, W_ih_scales, 0, 2 * H, 0, EARLY, range(1, 4))

        load_w(1, 1, 0, 1)
        load_x(1, 2)
        load_w(0, 2, 1, 2)
        load_sw(0, 1, EARLY, PASSES)
        load_x(2, 4)
        load_w(0, 1, 2, 4)
        load_sx(X_FIRST, PASSES)
        load_x(4, 6)
        load_w(0, 1, 4, 6)
        load_x(6, 8)
        load_w(0, 1, 6, 8)

        gh_sb = keep.tile([P, 3 * H], BF16, name="gh_sb")
        nc.sync.dma_start(out=gh_sb[:], in_=gh)

        load_sw(1, 1, EARLY, PASSES)
        load_w(1, 1, 2, 4)
        load_w(1, 1, 4, 8)
        load_sw(2, 1, 0, PASSES)
        load_w(2, 1, 0, 4)
        load_w(2, 1, 4, 8)

        warm_ps = psum.tile([P, H], F32, name="warm_ps", tag="bank7")
        for i in range(WARM_BEFORE):
            nc.tensor.matmul(out=warm_ps[:, 0:P], lhsT=ones[:], rhs=ones[:], start=True, stop=True)
        bias_ps = []
        for j in range(3):
            bp = psum.tile([P, H], F32, name="bias_ps%d" % j, tag="bank%d" % (4 + j))
            nc.tensor.matmul(out=bp[:], lhsT=ones[:], rhs=brow[:, j * H : (j + 1) * H], start=True, stop=True)
            bias_ps.append(bp)

        b_sb = [keep.tile([P, H], F32, name="b_sb%d" % j) for j in range(3)]
        nc.scalar.copy(out=b_sb[0][:], in_=bias_ps[0][:])
        nc.vector.tensor_copy(out=b_sb[1][:], in_=bias_ps[1][:])
        nc.scalar.copy(out=b_sb[2][:], in_=bias_ps[2][:])
        bn = b_sb[2]

        def mx(acc, gate, s, g, c0, c1):
            xt, xj = cx[g]
            wt, wj, wo = cw[gate][g]
            sxt, sxj = sx[g]
            swt, swj, so = sw[gate][g]
            nc.tensor.matmul_mx(
                out=acc[:],
                lhsT=xt[:, xj, 2 * P * s : 2 * P * (s + 1)].bitcast(FP4X4),
                lhsT_scale=sxt[:, sxj, P * s : P * (s + 1)],
                rhs=wt[:, wj, wo + 2 * c0 : wo + 2 * c1].bitcast(FP4X4),
                rhs_scale=swt[:, swj, so + c0 : so + c1],
                start=(g == 0),
                stop=(g == PASSES - 1),
            )

        def f32_tile(label):
            return keep.tile([P, H], F32, name=label)

        r_ps = [psum.tile([P, H], F32, name="r_ps%d" % s, tag="bank%d" % s) for s in range(STEPS)]
        z_ps = [psum.tile([P, H], F32, name="z_ps%d" % s, tag="bank%d" % (4 + s)) for s in range(STEPS)]
        for g in range(STREAMED):
            for s in range(STEPS):
                mx(r_ps[s], 0, s, g, 0, H)
            if g < EARLY:
                for s in range(STEPS):
                    mx(z_ps[s], 1, s, g, 0, H)
        for s in range(STEPS):
            for g in range(STREAMED, PASSES):
                mx(r_ps[s], 0, s, g, 0, H)

        ghb = []
        for j in range(2):
            t = keep.tile([P, H], F32, name="ghb%d" % j)
            nc.vector.tensor_tensor(out=t[:], in0=b_sb[j][:], in1=gh_sb[:, j * H : (j + 1) * H], op=ALU.add)
            ghb.append(t)

        r = []

        def reset_gate(s):
            rp = f32_tile("rp%d" % s)
            nc.vector.tensor_tensor(out=rp[:], in0=r_ps[s][:], in1=ghb[0][:], op=ALU.add)
            rs = f32_tile("r%d" % s)
            nc.scalar.activation(out=rs[:], in_=rp[:], func=ACT.Sigmoid)
            r.append(rs)

        t1 = [f32_tile("t1_%d" % s) for s in range(STEPS)]
        t2 = [f32_tile("t2_%d" % s) for s in range(STEPS)]

        def rh(s):
            nc.vector.tensor_tensor(out=t1[s][:], in0=r[s][:], in1=gh_sb[:, 2 * H : 3 * H], op=ALU.mult)

        def rhb(s):
            nc.vector.tensor_tensor(out=t2[s][:], in0=t1[s][:], in1=bn[:], op=ALU.add)

        reset_gate(0)
        for s in range(1, STEPS):
            reset_gate(s)
            rh(s - 1)
            if s >= 2:
                rhb(s - 2)
        rh(STEPS - 1)
        rhb(STEPS - 2)
        rhb(STEPS - 1)

        for g in range(EARLY, STREAMED):
            for s in range(STEPS):
                mx(z_ps[s], 1, s, g, 0, H)
        for s in range(STEPS):
            for g in range(STREAMED, PASSES):
                mx(z_ps[s], 1, s, g, 0, H)

        zc = []
        for s in range(STEPS):
            zp = f32_tile("zp%d" % s)
            nc.vector.tensor_tensor(out=zp[:], in0=z_ps[s][:], in1=ghb[1][:], op=ALU.add)
            zs = f32_tile("zc%d" % s)
            nc.scalar.activation(out=zs[:], in_=zp[:], func=ACT.Sigmoid, scale=-1.0)
            zc.append(zs)

        def cand_pre(acc, s, c0, c1):
            w = c1 - c0
            pre = keep.tile([P, w], F32, name="np%d_%d" % (s, c0))
            nc.vector.tensor_tensor(out=pre[:], in0=acc[:], in1=t2[s][:, c0:c1], op=ALU.add)
            cand = keep.tile([P, w], F32, name="n%d_%d" % (s, c0))
            nc.scalar.activation(out=cand[:], in_=pre[:], func=ACT.Tanh)
            return cand

        def finish(cand, s, c0, c1):
            h = keep.tile([P, c1 - c0], F32, name="h%d_%d" % (s, c0))
            nc.vector.tensor_tensor(out=h[:], in0=zc[s][:, c0:c1], in1=cand[:], op=ALU.mult)
            nc.sync.dma_start(out=out[:, s, c0:c1], in_=h[:])

        waiting = None
        for i, (s, c0, c1) in enumerate(CAND_GROUPS):
            acc = psum.tile([P, c1 - c0], F32, name="n_ps%d" % i, tag="bank%d" % i)
            for g in range(PASSES):
                mx(acc, 2, s, g, c0, c1)
            cand = cand_pre(acc, s, c0, c1)
            if waiting is not None:
                finish(*waiting)
            waiting = (cand, s, c0, c1)
        finish(*waiting)
